import numpy as np
import ml_dtypes


def mxq(x, axis, fmt="e4m3"):
    dtype, down = {"e4m3": (ml_dtypes.float8_e4m3fn, 7), "e5m2": (ml_dtypes.float8_e5m2, 14)}[fmt]
    v = np.moveaxis(np.asarray(x, np.float32).astype(ml_dtypes.bfloat16).astype(np.float64), axis, -1)
    blocks = v.reshape(v.shape[:-1] + (-1, 32))
    amax = np.abs(blocks).max(-1, keepdims=True)
    byte = np.maximum(np.where(amax > 0, np.frexp(amax)[1] - 1 + 127, 0) - down, 1)
    scale = np.exp2(byte - 127.0)
    codes = (blocks / scale).astype(np.float32).astype(dtype).astype(np.float64)
    return np.moveaxis((codes * scale).reshape(v.shape), -1, axis)


WIDE = False


def mx_kscale(k):
    if not WIDE:
        return np.ones(k)
    levels = np.array([10, -10, 5, -5, 0])
    a = np.random.permutation(np.resize(levels, k // 512 * 4)).reshape(k // 512, 4)
    idx = np.arange(k)
    return np.exp2(a[idx // 512, idx % 128 // 32])


BF16 = ml_dtypes.bfloat16


def bf(x):
    return np.asarray(x, np.float32).astype(BF16)


def f64(x):
    return np.asarray(x).astype(np.float64)


B, HP, WP, E, F, NH, WS = 2, 8, 16, 512, 16384, 16, 8
NWH, NWW = HP // WS, WP // WS
L, N = B * NWH * NWW, WS * WS
LN_EPS = 1e-5
ERF_TERMS = 100


def erf(z):
    z = np.clip(z, -6.0, 6.0)
    u = z * z
    c = np.cumprod(np.concatenate([[1.0], 2.0 / (2.0 * np.arange(1, ERF_TERMS) + 1.0)]))
    acc = np.full_like(u, c[-1])
    for cn in c[-2::-1]:
        acc *= u
        acc += cn
    return 2.0 / np.sqrt(np.pi) * z * np.exp(-u) * acc


def gelu(v):
    return 0.5 * v * (1.0 + erf(v / np.sqrt(2.0)))


def layernorm(x, g, b):
    mu = x.mean(-1, keepdims=True)
    var = ((x - mu) ** 2).mean(-1, keepdims=True)
    return (x - mu) / np.sqrt(var + LN_EPS) * g + b


def setup_inputs():
    s = mx_kscale(E)
    s = s / s.max()
    return {"y": bf(np.random.standard_normal((L, N, E)) * s),
            "w1": bf(np.random.standard_normal((F, E)) / np.sqrt(E) / s),
            "b1": bf(np.random.standard_normal(F) * 0.2),
            "w2": bf(np.random.standard_normal((E, F)) * 1.5 / np.sqrt(F)),
            "b2": bf(np.random.standard_normal(E) * 0.2),
            "ln2_g": bf(1.0 + 0.1 * np.random.standard_normal(E)),
            "ln2_b": bf(np.random.standard_normal(E) * 0.2)}


def reference(y, w1, b1, w2, b2, ln2_g, ln2_b):
    y = f64(y)
    h = gelu((mxq(y, 2, "e4m3") @ mxq(f64(w1), 1, "e4m3").T) + f64(b1))
    ffn = (mxq(h, 2, "e4m3") @ mxq(f64(w2), 1, "e4m3").T) + f64(b2)
    z = layernorm(y + ffn, f64(ln2_g), f64(ln2_b))
    z = z.reshape(B, NWH, NWW, WS, WS, E).transpose(0, 1, 3, 2, 4, 5)
    return z.reshape(B, HP * WP, E)

@@ -1,0 +1,288 @@
+from contextlib import ExitStack
+
+import concourse.mybir as mybir
+from concourse.masks import make_identity
+
+F32 = mybir.dt.float32
+BF16 = mybir.dt.bfloat16
+U32 = mybir.dt.uint32
+U8 = mybir.dt.uint8
+FP8X4 = mybir.dt.float8_e4m3fn_x4
+ACT = mybir.ActivationFunctionType
+ALU = mybir.AluOpType
+
+P = 128
+TOKENS = 256
+E = 512
+F = 16384
+K_PASS = 4 * P
+GROUPS = F // K_PASS
+TOKEN_TILES = TOKENS // P
+LN_EPS = 1e-5
+
+GROUPS_PER_LOAD = 2
+LOADS = GROUPS // GROUPS_PER_LOAD
+LOAD_BUFS = 4
+
+FLOPS = 2 * 2 * TOKENS * E * F
+
+
+def tile_swintransformerblock_pb_k_kernel(tc, y, w1, b1, w2, b2, ln2_g, ln2_b, out):
+    nc = tc.nc
+    with ExitStack() as ctx:
+        ctx.enter_context(tc.manual_schedule())
+        const = ctx.enter_context(tc.tile_pool(name="const", bufs=1))
+        w1_pool = ctx.enter_context(tc.tile_pool(name="w1_pool", bufs=LOAD_BUFS))
+        w2_pool = ctx.enter_context(tc.tile_pool(name="w2_pool", bufs=LOAD_BUFS))
+        work = ctx.enter_context(tc.tile_pool(name="work", bufs=3))
+        keep4 = ctx.enter_context(tc.tile_pool(name="keep4", bufs=4))
+        psum_acc = ctx.enter_context(tc.psum_pool(name="psum_acc", bufs=1))
+        psum_tr = ctx.enter_context(tc.psum_pool(name="psum_tr", bufs=4))
+        psum_h = ctx.enter_context(tc.psum_pool(name="psum_h", bufs=2))
+
+        y_view = y.rearrange("l n e -> (l n) e").rearrange("(a p) e -> p a e", p=P)
+        w1_view = w1.rearrange("(c m r) e -> m c (r e)", m=P, r=2)
+        w2_view = w2.rearrange("(j p) f -> p j f", p=P)
+        b1_view = b1.rearrange("(c x) -> c x", x=2 * P)
+
+        w1_loaded = {}
+        w2_loaded = {}
+
+        def load_weights(c):
+            w1_sb = w1_pool.tile([P, GROUPS_PER_LOAD * 2 * 2 * E], BF16, name="w1_sb")
+            nc.sync.dma_start(
+                out=w1_sb[:].rearrange("p (c x) -> p c x", x=2 * E),
+                in_=w1_view[:, 2 * GROUPS_PER_LOAD * c : 2 * GROUPS_PER_LOAD * (c + 1), :],
+            )
+            w2_sb = w2_pool.tile([P, 4 * GROUPS_PER_LOAD * K_PASS], BF16, name="w2_sb")
+            nc.sync.dma_start(
+                out=w2_sb[:].rearrange("p (j f) -> p j f", j=4),
+                in_=w2_view[:, :, GROUPS_PER_LOAD * K_PASS * c : GROUPS_PER_LOAD * K_PASS * (c + 1)],
+            )
+            w1_loaded[c] = w1_sb
+            w2_loaded[c] = w2_sb
+
+        y_sb = const.tile([P, TOKEN_TILES * E], BF16, name="y_sb")
+        nc.sync.dma_start(out=y_sb[:].rearrange("p (a e) -> p a e", e=E), in_=y_view)
+        for c in range(LOAD_BUFS - 1):
+            load_weights(c)
+
+        b1_rows = const.tile([P, 2 * P], BF16, name="b1_rows")
+        nc.vector.memset(b1_rows[:], 0.0)
+        nc.scalar.dma_start(out=b1_rows[0 : F // (2 * P), :], in_=b1_view)
+        vec_rows = const.tile([P, 3 * E], BF16, name="vec_rows")
+        nc.vector.memset(vec_rows[:], 0.0)
+        for i, vec in enumerate((b2, ln2_g, ln2_b)):
+            nc.scalar.dma_start(
+                out=vec_rows[0:1, E * i : E * (i + 1)], in_=vec.rearrange("(o e) -> o e", o=1)
+            )
+        ones = const.tile([P, P], BF16, name="ones")
+        nc.vector.memset(ones[:], 1.0)
+        eps = const.tile([P, 1], F32, name="eps")
+        nc.vector.memset(eps[:], LN_EPS)
+        ident = const.tile([P, P], F32, name="ident")
+        make_identity(nc, ident[:])
+
+        def transpose_bank(words, starts):
+            bank = psum_tr.tile([P, 4 * P], F32, name="bank", tag="tr")
+            for i, start in enumerate(starts):
+                nc.tensor.transpose(bank[:, P * i : P * (i + 1)], words[:, start : start + P], ident[:])
+            return bank
+
+        def copy_out(copy, grouped, half, bank):
+            copy(
+                out=grouped[:].bitcast(F32)[:, 4 * P * half : 4 * P * (half + 1)].rearrange(
+                    "p (s m u) -> p s m u", s=2, u=2
+                ),
+                in_=bank[:].rearrange("p (s u m) -> p s m u", s=2, u=2),
+            )
+
+        def quantise(grouped, columns, pool, name):
+            codes = pool.tile([P, columns], U32, name=name + "_codes", align_bytes=64)
+            scales = pool.tile([P, columns], U8, name=name + "_scales", align_bytes=64)
+            nc.vector.quantize_mx(out=codes[:].bitcast(FP8X4), scales=scales[:], in_=grouped[:])
+            return codes, scales
+
+        y_words = y_sb[:].bitcast(F32)
+        y_bank = psum_tr.tile([P, 4 * P], F32, name="y_bank", tag="tr")
+        for u in range(2):
+            for a in range(TOKEN_TILES):
+                nc.tensor.transpose(
+                    y_bank[:, TOKENS * u + P * a : TOKENS * u + P * (a + 1)],
+                    y_words[:, (E // 2) * a + P * u : (E // 2) * a + P * (u + 1)],
+                    ident[:],
+                )
+        y_grouped = const.tile([P, 4 * TOKENS], BF16, name="y_grouped", align_bytes=64)
+        nc.vector.tensor_copy(
+            out=y_grouped[:].bitcast(F32).rearrange("p (m u) -> p m u", u=2),
+            in_=y_bank[:].rearrange("p (u m) -> p m u", u=2),
+        )
+
+        b1_bank = psum_tr.tile([P, 4 * P], F32, name="b1_bank", tag="tr")
+        nc.tensor.transpose(b1_bank[:, 0:P], b1_rows[:].bitcast(F32), ident[:])
+        b1_col = const.tile([P, 4 * GROUPS], F32, name="b1_col")
+        nc.vector.tensor_copy(out=b1_col[:], in_=b1_bank[:, 0 : 2 * GROUPS].bitcast(BF16))
+
+        y_codes, y_scales = quantise(y_grouped, TOKENS, const, "y")
+
+        spread = []
+        for i in range(3):
+            spread_bank = psum_tr.tile([P, E], F32, name="spread_bank", tag="tr")
+            nc.tensor.matmul(
+                spread_bank[:], lhsT=ones[:], rhs=vec_rows[:, E * i : E * (i + 1)], start=True, stop=True
+            )
+            spread.append(spread_bank)
+        y_plus_b2 = const.tile([P, TOKEN_TILES * E], F32, name="y_plus_b2")
+        for a in range(TOKEN_TILES):
+            nc.vector.tensor_tensor(
+                out=y_plus_b2[:, E * a : E * (a + 1)],
+                in0=y_sb[:, E * a : E * (a + 1)],
+                in1=spread[0][:],
+                op=ALU.add,
+            )
+        gain = const.tile([P, E], F32, name="gain")
+        nc.scalar.copy(out=gain[:], in_=spread[1][:])
+        shift = const.tile([P, E], F32, name="shift")
+        nc.scalar.copy(out=shift[:], in_=spread[2][:])
+
+        acc = []
+        for a in range(TOKEN_TILES):
+            acc_bank = psum_acc.tile([P, E], F32, name="acc%d" % a)
+            acc.append(acc_bank)
+
+        banks = {}
+        w1_grouped = {}
+        w2_grouped = {}
+        w1_q = {}
+        w2_q = {}
+        h_banks = {}
+        h_planes = {}
+        h_grouped = {}
+        h_q = {}
+
+        def transposes(g):
+            c, gl = divmod(g, GROUPS_PER_LOAD)
+            w1_words = w1_loaded[c][:].bitcast(F32)
+            w2_words = w2_loaded[c][:].bitcast(F32)
+            four = []
+            for u in range(2):
+                base = (2 * gl + u) * E
+                four.append(transpose_bank(w1_words, [base + P * i for i in range(4)]))
+            row = GROUPS_PER_LOAD * K_PASS // 2
+            for half in range(2):
+                starts = [
+                    row * (2 * half + s) + (K_PASS // 2) * gl + P * u for s in range(2) for u in range(2)
+                ]
+                four.append(transpose_bank(w2_words, starts))
+            banks[g] = four
+
+        def copy_outs_scalar(g):
+            w1_g = work.tile([P, 4 * K_PASS], BF16, name="w1_g", align_bytes=64)
+            w2_g = work.tile([P, 4 * K_PASS], BF16, name="w2_g", align_bytes=64)
+            w1_grouped[g] = w1_g
+            w2_grouped[g] = w2_g
+            copy_out(nc.scalar.copy, w1_g, 0, banks[g][0])
+            copy_out(nc.scalar.copy, w1_g, 1, banks[g][1])
+            copy_out(nc.scalar.copy, w2_g, 0, banks[g][2])
+
+        def copy_out_vector(g):
+            copy_out(nc.vector.tensor_copy, w2_grouped[g], 1, banks[g][3])
+
+        def matmul1(g):
+            codes, scales = w1_q[g]
+            pair = []
+            for half in range(2):
+                h_bank = psum_h.tile([P, 2 * TOKENS], F32, name="h_bank", tag="hp")
+                for s in range(2):
+                    t = 2 * half + s
+                    nc.tensor.matmul_mx(
+                        out=h_bank[:, TOKENS * s : TOKENS * (s + 1)],
+                        lhsT=codes[:, P * t : P * (t + 1)].bitcast(FP8X4),
+                        lhsT_scale=scales[:, P * t : P * (t + 1)],
+                        rhs=y_codes[:].bitcast(FP8X4),
+                        rhs_scale=y_scales[:],
+                        start=True,
+                        stop=True,
+                    )
+                pair.append(h_bank)
+            h_banks[g] = pair
+
+        def gelu(g):
+            planes = work.tile([P, 4 * TOKENS], BF16, name="planes")
+            for t in range(4):
+                nc.scalar.activation(
+                    out=planes[:, TOKENS * t : TOKENS * (t + 1)],
+                    in_=h_banks[g][t // 2][:, TOKENS * (t % 2) : TOKENS * (t % 2 + 1)],
+                    func=ACT.Gelu,
+                    bias=b1_col[:, 4 * g + t : 4 * g + t + 1],
+                    scale=1.0,
+                )
+            h_planes[g] = planes
+
+        def regroup(g):
+            h_g = work.tile([P, 4 * TOKENS], BF16, name="h_g", align_bytes=64)
+            nc.vector.tensor_copy(
+                out=h_g[:].rearrange("p (c i t) -> p c t i", i=4, t=4),
+                in_=h_planes[g][:].rearrange("p (t c i) -> p c t i", i=4, t=4),
+            )
+            h_grouped[g] = h_g
+
+        def matmul2(g):
+            h_codes, h_scales = h_q[g]
+            w2_codes, w2_scales = w2_q[g]
+            for a in range(TOKEN_TILES):
+                nc.tensor.matmul_mx(
+                    out=acc[a][:],
+                    lhsT=h_codes[:, P * a : P * (a + 1)].bitcast(FP8X4),
+                    lhsT_scale=h_scales[:, P * a : P * (a + 1)],
+                    rhs=w2_codes[:].bitcast(FP8X4),
+                    rhs_scale=w2_scales[:],
+                    start=(g == 0),
+                    stop=(g == GROUPS - 1),
+                )
+
+        for j in range(GROUPS + 3):
+            if j % GROUPS_PER_LOAD == 0 and j // GROUPS_PER_LOAD + LOAD_BUFS - 1 < LOADS:
+                load_weights(j // GROUPS_PER_LOAD + LOAD_BUFS - 1)
+            if j < GROUPS:
+                transposes(j)
+            if 0 <= j - 1 < GROUPS:
+                w1_q[j - 1] = quantise(w1_grouped[j - 1], K_PASS, work, "w1")
+                matmul1(j - 1)
+            if 0 <= j - 3 < GROUPS:
+                matmul2(j - 3)
+            if j < GROUPS:
+                copy_outs_scalar(j)
+            if 0 <= j - 2 < GROUPS:
+                regroup(j - 2)
+            if j < GROUPS:
+                copy_out_vector(j)
+            if 0 <= j - 1 < GROUPS:
+                gelu(j - 1)
+            if 0 <= j - 2 < GROUPS:
+                h_q[j - 2] = quantise(h_grouped[j - 2], TOKENS, work, "h")
+            if 0 <= j - 1 < GROUPS:
+                w2_q[j - 1] = quantise(w2_grouped[j - 1], K_PASS, keep4, "w2")
+
+        for a in range(TOKEN_TILES):
+            r = work.tile([P, E], F32, name="r")
+            nc.vector.tensor_tensor(out=r[:], in0=acc[a][:], in1=y_plus_b2[:, E * a : E * (a + 1)], op=ALU.add)
+            stats = work.tile([P, 6], F32, name="stats")
+            nc.vector.bn_stats(out=stats[:], in_=r[:])
+            mean_var = work.tile([P, 2], F32, name="mean_var")
+            nc.vector.bn_aggr(out=mean_var[:], in_=stats[:])
+            std = work.tile([P, 1], F32, name="std")
+            nc.scalar.activation(out=std[:], in_=mean_var[:, 1:2], func=ACT.Sqrt, bias=eps[:], scale=1.0)
+            rstd = work.tile([P, 1], F32, name="rstd")
+            nc.vector.reciprocal(out=rstd[:], in_=std[:])
+            centred = work.tile([P, E], F32, name="centred")
+            nc.vector.scalar_tensor_tensor(
+                out=centred[:], in0=r[:], scalar=mean_var[:, 0:1], in1=gain[:], op0=ALU.subtract, op1=ALU.mult
+            )
+            z = work.tile([P, E], F32, name="z")
+            nc.vector.scalar_tensor_tensor(
+                out=z[:], in0=centred[:], scalar=rstd[:], in1=shift[:], op0=ALU.mult, op1=ALU.add
+            )
+            patches = out[a].rearrange("(r w c) e -> w r c e", w=2, c=8)
+            for w in range(2):
+                nc.sync.dma_start(out=patches[w], in_=z[64 * w : 64 * (w + 1), :])

@@ -20,9 +20,10 @@ GROUPS = F // K_PASS
 TOKEN_TILES = TOKENS // P
 LN_EPS = 1e-5
 
-GROUPS_PER_LOAD = 2
-LOADS = GROUPS // GROUPS_PER_LOAD
-LOAD_BUFS = 4
+W2_LAG = 2
+W2_GROUPS_PER_LOAD = 2
+LOADS_AHEAD = 6
+VECTOR_EVERY = 4
 
 FLOPS = 2 * 2 * TOKENS * E * F
 
@@ -32,41 +33,39 @@ def tile_swintransformerblock_pb_k_kernel(tc, y, w1, b1, w2, b2, ln2_g, ln2_b, o
     with ExitStack() as ctx:
         ctx.enter_context(tc.manual_schedule())
         const = ctx.enter_context(tc.tile_pool(name="const", bufs=1))
-        w1_pool = ctx.enter_context(tc.tile_pool(name="w1_pool", bufs=LOAD_BUFS))
-        w2_pool = ctx.enter_context(tc.tile_pool(name="w2_pool", bufs=LOAD_BUFS))
+        w1_pool = ctx.enter_context(tc.tile_pool(name="w1_pool", bufs=LOADS_AHEAD))
+        w2_pool = ctx.enter_context(tc.tile_pool(name="w2_pool", bufs=4))
         work = ctx.enter_context(tc.tile_pool(name="work", bufs=3))
-        keep4 = ctx.enter_context(tc.tile_pool(name="keep4", bufs=4))
         psum_acc = ctx.enter_context(tc.psum_pool(name="psum_acc", bufs=1))
         psum_tr = ctx.enter_context(tc.psum_pool(name="psum_tr", bufs=4))
         psum_h = ctx.enter_context(tc.psum_pool(name="psum_h", bufs=2))
 
         y_view = y.rearrange("l n e -> (l n) e").rearrange("(a p) e -> p a e", p=P)
-        w1_view = w1.rearrange("(c m r) e -> m c (r e)", m=P, r=2)
+        w1_view = w1.rearrange("(g u m r) e -> g m u (r e)", u=2, m=P, r=2)
         w2_view = w2.rearrange("(j p) f -> p j f", p=P)
         b1_view = b1.rearrange("(c x) -> c x", x=2 * P)
 
         w1_loaded = {}
         w2_loaded = {}
 
-        def load_weights(c):
-            w1_sb = w1_pool.tile([P, GROUPS_PER_LOAD * 2 * 2 * E], BF16, name="w1_sb")
-            nc.sync.dma_start(
-                out=w1_sb[:].rearrange("p (c x) -> p c x", x=2 * E),
-                in_=w1_view[:, 2 * GROUPS_PER_LOAD * c : 2 * GROUPS_PER_LOAD * (c + 1), :],
-            )
-            w2_sb = w2_pool.tile([P, 4 * GROUPS_PER_LOAD * K_PASS], BF16, name="w2_sb")
-            nc.sync.dma_start(
-                out=w2_sb[:].rearrange("p (j f) -> p j f", j=4),
-                in_=w2_view[:, :, GROUPS_PER_LOAD * K_PASS * c : GROUPS_PER_LOAD * K_PASS * (c + 1)],
-            )
-            w1_loaded[c] = w1_sb
-            w2_loaded[c] = w2_sb
+        def load_round(j):
+            if j < GROUPS:
+                w1_sb = w1_pool.tile([P, 2 * 2 * E], BF16, name="w1_sb")
+                nc.sync.dma_start(out=w1_sb[:].rearrange("p (u x) -> p u x", u=2), in_=w1_view[j])
+                w1_loaded[j] = w1_sb
+            g = j - W2_LAG
+            if 0 <= g < GROUPS and g % W2_GROUPS_PER_LOAD == 0:
+                w2_sb = w2_pool.tile([P, 4 * W2_GROUPS_PER_LOAD * K_PASS], BF16, name="w2_sb")
+                nc.sync.dma_start(
+                    out=w2_sb[:].rearrange("p (j f) -> p j f", j=4),
+                    in_=w2_view[:, :, K_PASS * g : K_PASS * (g + W2_GROUPS_PER_LOAD)],
+                )
+                w2_loaded[g // W2_GROUPS_PER_LOAD] = w2_sb
 
+        for j in range(LOADS_AHEAD):
+            load_round(j)
         y_sb = const.tile([P, TOKEN_TILES * E], BF16, name="y_sb")
-        nc.sync.dma_start(out=y_sb[:].rearrange("p (a e) -> p a e", e=E), in_=y_view)
-        for c in range(LOAD_BUFS - 1):
-            load_weights(c)
-
+        nc.scalar.dma_start(out=y_sb[:].rearrange("p (a e) -> p a e", e=E), in_=y_view)
         b1_rows = const.tile([P, 2 * P], BF16, name="b1_rows")
         nc.vector.memset(b1_rows[:], 0.0)
         nc.scalar.dma_start(out=b1_rows[0 : F // (2 * P), :], in_=b1_view)
@@ -125,32 +124,35 @@ def tile_swintransformerblock_pb_k_kernel(tc, y, w1, b1, w2, b2, ln2_g, ln2_b, o
 
         y_codes, y_scales = quantise(y_grouped, TOKENS, const, "y")
 
-        spread = []
-        for i in range(3):
-            spread_bank = psum_tr.tile([P, E], F32, name="spread_bank", tag="tr")
-            nc.tensor.matmul(
-                spread_bank[:], lhsT=ones[:], rhs=vec_rows[:, E * i : E * (i + 1)], start=True, stop=True
-            )
-            spread.append(spread_bank)
         y_plus_b2 = const.tile([P, TOKEN_TILES * E], F32, name="y_plus_b2")
-        for a in range(TOKEN_TILES):
-            nc.vector.tensor_tensor(
-                out=y_plus_b2[:, E * a : E * (a + 1)],
-                in0=y_sb[:, E * a : E * (a + 1)],
-                in1=spread[0][:],
-                op=ALU.add,
-            )
         gain = const.tile([P, E], F32, name="gain")
-        nc.scalar.copy(out=gain[:], in_=spread[1][:])
         shift = const.tile([P, E], F32, name="shift")
-        nc.scalar.copy(out=shift[:], in_=spread[2][:])
+
+        def spread_vectors():
+            spread = []
+            for i in range(3):
+                spread_bank = psum_tr.tile([P, E], F32, name="spread_bank", tag="tr")
+                nc.tensor.matmul(
+                    spread_bank[:], lhsT=ones[:], rhs=vec_rows[:, E * i : E * (i + 1)], start=True, stop=True
+                )
+                spread.append(spread_bank)
+            for a in range(TOKEN_TILES):
+                nc.vector.tensor_tensor(
+                    out=y_plus_b2[:, E * a : E * (a + 1)],
+                    in0=y_sb[:, E * a : E * (a + 1)],
+                    in1=spread[0][:],
+                    op=ALU.add,
+                )
+            nc.scalar.copy(out=gain[:], in_=spread[1][:])
+            nc.scalar.copy(out=shift[:], in_=spread[2][:])
 
         acc = []
         for a in range(TOKEN_TILES):
             acc_bank = psum_acc.tile([P, E], F32, name="acc%d" % a)
             acc.append(acc_bank)
 
-        banks = {}
+        w1_banks = {}
+        w2_banks = {}
         w1_grouped = {}
         w2_grouped = {}
         w1_q = {}
@@ -160,33 +162,25 @@ def tile_swintransformerblock_pb_k_kernel(tc, y, w1, b1, w2, b2, ln2_g, ln2_b, o
         h_grouped = {}
         h_q = {}
 
-        def transposes(g):
-            c, gl = divmod(g, GROUPS_PER_LOAD)
-            w1_words = w1_loaded[c][:].bitcast(F32)
-            w2_words = w2_loaded[c][:].bitcast(F32)
-            four = []
-            for u in range(2):
-                base = (2 * gl + u) * E
-                four.append(transpose_bank(w1_words, [base + P * i for i in range(4)]))
-            row = GROUPS_PER_LOAD * K_PASS // 2
-            for half in range(2):
-                starts = [
-                    row * (2 * half + s) + (K_PASS // 2) * gl + P * u for s in range(2) for u in range(2)
-                ]
-                four.append(transpose_bank(w2_words, starts))
-            banks[g] = four
-
-        def copy_outs_scalar(g):
+        def transpose_w1(g):
+            words = w1_loaded[g][:].bitcast(F32)
+            w1_banks[g] = [transpose_bank(words, [E * u + P * i for i in range(4)]) for u in range(2)]
             w1_g = work.tile([P, 4 * K_PASS], BF16, name="w1_g", align_bytes=64)
-            w2_g = work.tile([P, 4 * K_PASS], BF16, name="w2_g", align_bytes=64)
             w1_grouped[g] = w1_g
-            w2_grouped[g] = w2_g
-            copy_out(nc.scalar.copy, w1_g, 0, banks[g][0])
-            copy_out(nc.scalar.copy, w1_g, 1, banks[g][1])
-            copy_out(nc.scalar.copy, w2_g, 0, banks[g][2])
 
-        def copy_out_vector(g):
-            copy_out(nc.vector.tensor_copy, w2_grouped[g], 1, banks[g][3])
+        def transpose_w2(g):
+            c, gl = divmod(g, W2_GROUPS_PER_LOAD)
+            words = w2_loaded[c][:].bitcast(F32)
+            row = W2_GROUPS_PER_LOAD * K_PASS // 2
+            w2_banks[g] = [
+                transpose_bank(
+                    words,
+                    [row * (2 * half + s) + (K_PASS // 2) * gl + P * u for s in range(2) for u in range(2)],
+                )
+                for half in range(2)
+            ]
+            w2_g = work.tile([P, 4 * K_PASS], BF16, name="w2_g", align_bytes=64)
+            w2_grouped[g] = w2_g
 
         def matmul1(g):
             codes, scales = w1_q[g]
@@ -241,45 +235,79 @@ def tile_swintransformerblock_pb_k_kernel(tc, y, w1, b1, w2, b2, ln2_g, ln2_b, o
                     stop=(g == GROUPS - 1),
                 )
 
-        for j in range(GROUPS + 3):
-            if j % GROUPS_PER_LOAD == 0 and j // GROUPS_PER_LOAD + LOAD_BUFS - 1 < LOADS:
-                load_weights(j // GROUPS_PER_LOAD + LOAD_BUFS - 1)
-            if j < GROUPS:
-                transposes(j)
-            if 0 <= j - 1 < GROUPS:
+        def live(g):
+            return 0 <= g < GROUPS
+
+        for j in range(GROUPS + W2_LAG + 1):
+            g2 = j - W2_LAG
+            if live(j):
+                transpose_w1(j)
+            if live(g2):
+                transpose_w2(g2)
+            load_round(j + LOADS_AHEAD)
+            if live(g2 - 1):
+                w2_q[g2 - 1] = quantise(w2_grouped[g2 - 1], K_PASS, work, "w2")
+            if live(j - 1):
                 w1_q[j - 1] = quantise(w1_grouped[j - 1], K_PASS, work, "w1")
                 matmul1(j - 1)
-            if 0 <= j - 3 < GROUPS:
-                matmul2(j - 3)
-            if j < GROUPS:
-                copy_outs_scalar(j)
-            if 0 <= j - 2 < GROUPS:
+            if live(g2 - 1):
+                matmul2(g2 - 1)
+            if live(j - 2):
                 regroup(j - 2)
-            if j < GROUPS:
-                copy_out_vector(j)
-            if 0 <= j - 1 < GROUPS:
+            if live(j):
+                copy_out(nc.scalar.copy, w1_grouped[j], 0, w1_banks[j][0])
+                copy_out(nc.vector.tensor_copy, w1_grouped[j], 1, w1_banks[j][1])
+            if live(g2):
+                copy_out(nc.scalar.copy, w2_grouped[g2], 0, w2_banks[g2][0])
+                if g2 % VECTOR_EVERY == 0:
+                    copy_out(nc.vector.tensor_copy, w2_grouped[g2], 1, w2_banks[g2][1])
+                else:
+                    copy_out(nc.scalar.copy, w2_grouped[g2], 1, w2_banks[g2][1])
+            if live(j - 1):
                 gelu(j - 1)
-            if 0 <= j - 2 < GROUPS:
+            if live(j - 2):
                 h_q[j - 2] = quantise(h_grouped[j - 2], TOKENS, work, "h")
-            if 0 <= j - 1 < GROUPS:
-                w2_q[j - 1] = quantise(w2_grouped[j - 1], K_PASS, keep4, "w2")
+            if j == 1:
+                spread_vectors()
 
+        warm = const.tile([P, 1], F32, name="warm")
+        nc.scalar.activation(out=warm[:], in_=eps[:], func=ACT.Sqrt)
+        r = []
+        neg_mean = []
         for a in range(TOKEN_TILES):
-            r = work.tile([P, E], F32, name="r")
-            nc.vector.tensor_tensor(out=r[:], in0=acc[a][:], in1=y_plus_b2[:, E * a : E * (a + 1)], op=ALU.add)
-            stats = work.tile([P, 6], F32, name="stats")
-            nc.vector.bn_stats(out=stats[:], in_=r[:])
-            mean_var = work.tile([P, 2], F32, name="mean_var")
-            nc.vector.bn_aggr(out=mean_var[:], in_=stats[:])
-            std = work.tile([P, 1], F32, name="std")
-            nc.scalar.activation(out=std[:], in_=mean_var[:, 1:2], func=ACT.Sqrt, bias=eps[:], scale=1.0)
-            rstd = work.tile([P, 1], F32, name="rstd")
-            nc.vector.reciprocal(out=rstd[:], in_=std[:])
-            centred = work.tile([P, E], F32, name="centred")
+            r_a = const.tile([P, E], F32, name="r%d" % a)
+            row_sum = const.tile([P, 1], F32, name="row_sum%d" % a)
             nc.vector.scalar_tensor_tensor(
-                out=centred[:], in0=r[:], scalar=mean_var[:, 0:1], in1=gain[:], op0=ALU.subtract, op1=ALU.mult
+                out=r_a[:],
+                in0=acc[a][:],
+                scalar=1.0,
+                in1=y_plus_b2[:, E * a : E * (a + 1)],
+                op0=ALU.mult,
+                op1=ALU.add,
+                accum_out=row_sum[:],
             )
-            z = work.tile([P, E], F32, name="z")
+            neg_mean_a = const.tile([P, 1], F32, name="neg_mean%d" % a)
+            nc.vector.tensor_scalar(
+                out=neg_mean_a[:], in0=row_sum[:], scalar1=-1.0 / E, scalar2=None, op0=ALU.mult
+            )
+            r.append(r_a)
+            neg_mean.append(neg_mean_a)
+        for a in range(TOKEN_TILES):
+            squares = const.tile([P, E], F32, name="squares%d" % a)
+            sum_squares = const.tile([P, 1], F32, name="sum_squares%d" % a)
+            nc.scalar.activation(
+                out=squares[:], in_=r[a][:], func=ACT.Square, bias=neg_mean[a][:], scale=1.0,
+                accum_out=sum_squares[:],
+            )
+            std = const.tile([P, 1], F32, name="std%d" % a)
+            nc.scalar.activation(out=std[:], in_=sum_squares[:], func=ACT.Sqrt, bias=eps[:], scale=1.0 / E)
+            centred = const.tile([P, E], F32, name="centred%d" % a)
+            nc.vector.scalar_tensor_tensor(
+                out=centred[:], in0=r[a][:], scalar=neg_mean[a][:], in1=gain[:], op0=ALU.add, op1=ALU.mult
+            )
+            rstd = const.tile([P, 1], F32, name="rstd%d" % a)
+            nc.vector.reciprocal(out=rstd[:], in_=std[:])
+            z = const.tile([P, E], F32, name="z%d" % a)
             nc.vector.scalar_tensor_tensor(
                 out=z[:], in0=centred[:], scalar=rstd[:], in1=shift[:], op0=ALU.mult, op1=ALU.add
             )

@@ -23,7 +23,6 @@ LN_EPS = 1e-5
 W2_LAG = 2
 W2_GROUPS_PER_LOAD = 2
 LOADS_AHEAD = 6
-VECTOR_EVERY = 4
 
 FLOPS = 2 * 2 * TOKENS * E * F
 
@@ -88,9 +87,9 @@ def tile_swintransformerblock_pb_k_kernel(tc, y, w1, b1, w2, b2, ln2_g, ln2_b, o
                 nc.tensor.transpose(bank[:, P * i : P * (i + 1)], words[:, start : start + P], ident[:])
             return bank
 
-        def copy_out(copy, grouped, half, bank):
+        def copy_out(copy, grouped, quarter, bank):
             copy(
-                out=grouped[:].bitcast(F32)[:, 4 * P * half : 4 * P * (half + 1)].rearrange(
+                out=grouped[:].bitcast(F32)[:, 4 * P * quarter : 4 * P * (quarter + 1)].rearrange(
                     "p (s m u) -> p s m u", s=2, u=2
                 ),
                 in_=bank[:].rearrange("p (s u m) -> p s m u", s=2, u=2),
@@ -153,10 +152,8 @@ def tile_swintransformerblock_pb_k_kernel(tc, y, w1, b1, w2, b2, ln2_g, ln2_b, o
 
         w1_banks = {}
         w2_banks = {}
-        w1_grouped = {}
-        w2_grouped = {}
-        w1_q = {}
-        w2_q = {}
+        grouped = {}
+        weights_q = {}
         h_banks = {}
         h_planes = {}
         h_grouped = {}
@@ -165,8 +162,6 @@ def tile_swintransformerblock_pb_k_kernel(tc, y, w1, b1, w2, b2, ln2_g, ln2_b, o
         def transpose_w1(g):
             words = w1_loaded[g][:].bitcast(F32)
             w1_banks[g] = [transpose_bank(words, [E * u + P * i for i in range(4)]) for u in range(2)]
-            w1_g = work.tile([P, 4 * K_PASS], BF16, name="w1_g", align_bytes=64)
-            w1_grouped[g] = w1_g
 
         def transpose_w2(g):
             c, gl = divmod(g, W2_GROUPS_PER_LOAD)
@@ -179,11 +174,21 @@ def tile_swintransformerblock_pb_k_kernel(tc, y, w1, b1, w2, b2, ln2_g, ln2_b, o
                 )
                 for half in range(2)
             ]
-            w2_g = work.tile([P, 4 * K_PASS], BF16, name="w2_g", align_bytes=64)
-            w2_grouped[g] = w2_g
+
+        def quantise_weights(j):
+            codes = work.tile([P, 2 * K_PASS], U32, name="w_codes", align_bytes=64)
+            scales = work.tile([P, 2 * K_PASS], U8, name="w_scales", align_bytes=64)
+            first = 0 if live(j) else K_PASS
+            last = 2 * K_PASS if live(j - W2_LAG) else K_PASS
+            nc.vector.quantize_mx(
+                out=codes[:, first:last].bitcast(FP8X4),
+                scales=scales[:, first:last],
+                in_=grouped[j][:, 4 * first : 4 * last],
+            )
+            weights_q[j] = (codes, scales)
 
         def matmul1(g):
-            codes, scales = w1_q[g]
+            codes, scales = weights_q[g]
             pair = []
             for half in range(2):
                 h_bank = psum_h.tile([P, 2 * TOKENS], F32, name="h_bank", tag="hp")
@@ -223,14 +228,14 @@ def tile_swintransformerblock_pb_k_kernel(tc, y, w1, b1, w2, b2, ln2_g, ln2_b, o
 
         def matmul2(g):
             h_codes, h_scales = h_q[g]
-            w2_codes, w2_scales = w2_q[g]
+            w_codes, w_scales = weights_q[g + W2_LAG]
             for a in range(TOKEN_TILES):
                 nc.tensor.matmul_mx(
                     out=acc[a][:],
                     lhsT=h_codes[:, P * a : P * (a + 1)].bitcast(FP8X4),
                     lhsT_scale=h_scales[:, P * a : P * (a + 1)],
-                    rhs=w2_codes[:].bitcast(FP8X4),
-                    rhs_scale=w2_scales[:],
+                    rhs=w_codes[:, K_PASS : 2 * K_PASS].bitcast(FP8X4),
+                    rhs_scale=w_scales[:, K_PASS : 2 * K_PASS],
                     start=(g == 0),
                     stop=(g == GROUPS - 1),
                 )
@@ -245,24 +250,23 @@ def tile_swintransformerblock_pb_k_kernel(tc, y, w1, b1, w2, b2, ln2_g, ln2_b, o
             if live(g2):
                 transpose_w2(g2)
             load_round(j + LOADS_AHEAD)
-            if live(g2 - 1):
-                w2_q[g2 - 1] = quantise(w2_grouped[g2 - 1], K_PASS, work, "w2")
+            if live(j - 1) or live(g2 - 1):
+                quantise_weights(j - 1)
             if live(j - 1):
-                w1_q[j - 1] = quantise(w1_grouped[j - 1], K_PASS, work, "w1")
                 matmul1(j - 1)
             if live(g2 - 1):
                 matmul2(g2 - 1)
             if live(j - 2):
                 regroup(j - 2)
+            if live(j) or live(g2):
+                round_grouped = work.tile([P, 8 * K_PASS], BF16, name="round_grouped", align_bytes=64)
+                grouped[j] = round_grouped
             if live(j):
-                copy_out(nc.scalar.copy, w1_grouped[j], 0, w1_banks[j][0])
-                copy_out(nc.vector.tensor_copy, w1_grouped[j], 1, w1_banks[j][1])
+                copy_out(nc.scalar.copy, round_grouped, 0, w1_banks[j][0])
+                copy_out(nc.vector.tensor_copy, round_grouped, 1, w1_banks[j][1])
             if live(g2):
-                copy_out(nc.scalar.copy, w2_grouped[g2], 0, w2_banks[g2][0])
-                if g2 % VECTOR_EVERY == 0:
-                    copy_out(nc.vector.tensor_copy, w2_grouped[g2], 1, w2_banks[g2][1])
-                else:
-                    copy_out(nc.scalar.copy, w2_grouped[g2], 1, w2_banks[g2][1])
+                copy_out(nc.scalar.copy, round_grouped, 2, w2_banks[g2][0])
+                copy_out(nc.scalar.copy, round_grouped, 3, w2_banks[g2][1])
             if live(j - 1):
                 gelu(j - 1)
             if live(j - 2):

@@ -50,21 +50,32 @@ def tile_swintransformerblock_pb_k_kernel(tc, y, w1, b1, w2, b2, ln2_g, ln2_b, o
         def load_round(j):
             if j < GROUPS:
                 w1_sb = w1_pool.tile([P, 2 * 2 * E], BF16, name="w1_sb")
-                nc.sync.dma_start(out=w1_sb[:].rearrange("p (u x) -> p u x", u=2), in_=w1_view[j])
+                if j == 0:
+                    for u in range(2):
+                        nc.sync.dma_start(out=w1_sb[:, 2 * E * u : 2 * E * (u + 1)], in_=w1_view[j][:, u, :])
+                else:
+                    nc.sync.dma_start(out=w1_sb[:].rearrange("p (u x) -> p u x", u=2), in_=w1_view[j])
                 w1_loaded[j] = w1_sb
             g = j - W2_LAG
             if 0 <= g < GROUPS and g % W2_GROUPS_PER_LOAD == 0:
                 w2_sb = w2_pool.tile([P, 4 * W2_GROUPS_PER_LOAD * K_PASS], BF16, name="w2_sb")
+                w2_loaded[g // W2_GROUPS_PER_LOAD] = w2_sb
+            if 0 <= g < W2_GROUPS_PER_LOAD:
                 nc.sync.dma_start(
-                    out=w2_sb[:].rearrange("p (j f) -> p j f", j=4),
+                    out=w2_loaded[0][:].rearrange("p (j f) -> p j f", j=4)[:, :, K_PASS * g : K_PASS * (g + 1)],
+                    in_=w2_view[:, :, K_PASS * g : K_PASS * (g + 1)],
+                )
+            elif W2_GROUPS_PER_LOAD <= g < GROUPS and g % W2_GROUPS_PER_LOAD == 0:
+                nc.sync.dma_start(
+                    out=w2_loaded[g // W2_GROUPS_PER_LOAD][:].rearrange("p (j f) -> p j f", j=4),
                     in_=w2_view[:, :, K_PASS * g : K_PASS * (g + W2_GROUPS_PER_LOAD)],
                 )
-                w2_loaded[g // W2_GROUPS_PER_LOAD] = w2_sb
 
-        for j in range(LOADS_AHEAD):
-            load_round(j)
+        load_round(0)
         y_sb = const.tile([P, TOKEN_TILES * E], BF16, name="y_sb")
-        nc.scalar.dma_start(out=y_sb[:].rearrange("p (a e) -> p a e", e=E), in_=y_view)
+        nc.sync.dma_start(out=y_sb[:].rearrange("p (a e) -> p a e", e=E), in_=y_view)
+        for j in range(1, LOADS_AHEAD):
+            load_round(j)
         b1_rows = const.tile([P, 2 * P], BF16, name="b1_rows")
         nc.vector.memset(b1_rows[:], 0.0)
         nc.scalar.dma_start(out=b1_rows[0 : F // (2 * P), :], in_=b1_view)
@@ -80,6 +91,8 @@ def tile_swintransformerblock_pb_k_kernel(tc, y, w1, b1, w2, b2, ln2_g, ln2_b, o
         nc.vector.memset(eps[:], LN_EPS)
         ident = const.tile([P, P], F32, name="ident")
         make_identity(nc, ident[:])
+        warm_gelu = const.tile([P, 1], F32, name="warm_gelu")
+        nc.scalar.activation(out=warm_gelu[:], in_=eps[:], func=ACT.Gelu)
 
         def transpose_bank(words, starts):
             bank = psum_tr.tile([P, 4 * P], F32, name="bank", tag="tr")
@@ -101,27 +114,29 @@ def tile_swintransformerblock_pb_k_kernel(tc, y, w1, b1, w2, b2, ln2_g, ln2_b, o
             nc.vector.quantize_mx(out=codes[:].bitcast(FP8X4), scales=scales[:], in_=grouped[:])
             return codes, scales
 
-        y_words = y_sb[:].bitcast(F32)
-        y_bank = psum_tr.tile([P, 4 * P], F32, name="y_bank", tag="tr")
-        for u in range(2):
-            for a in range(TOKEN_TILES):
-                nc.tensor.transpose(
-                    y_bank[:, TOKENS * u + P * a : TOKENS * u + P * (a + 1)],
-                    y_words[:, (E // 2) * a + P * u : (E // 2) * a + P * (u + 1)],
-                    ident[:],
-                )
         y_grouped = const.tile([P, 4 * TOKENS], BF16, name="y_grouped", align_bytes=64)
-        nc.vector.tensor_copy(
-            out=y_grouped[:].bitcast(F32).rearrange("p (m u) -> p m u", u=2),
-            in_=y_bank[:].rearrange("p (u m) -> p m u", u=2),
-        )
-
-        b1_bank = psum_tr.tile([P, 4 * P], F32, name="b1_bank", tag="tr")
-        nc.tensor.transpose(b1_bank[:, 0:P], b1_rows[:].bitcast(F32), ident[:])
         b1_col = const.tile([P, 4 * GROUPS], F32, name="b1_col")
-        nc.vector.tensor_copy(out=b1_col[:], in_=b1_bank[:, 0 : 2 * GROUPS].bitcast(BF16))
+        y_codes = const.tile([P, TOKENS], U32, name="y_codes", align_bytes=64)
+        y_scales = const.tile([P, TOKENS], U8, name="y_scales", align_bytes=64)
 
-        y_codes, y_scales = quantise(y_grouped, TOKENS, const, "y")
+        def prepare_y_and_b1():
+            y_words = y_sb[:].bitcast(F32)
+            y_bank = psum_tr.tile([P, 4 * P], F32, name="y_bank", tag="tr")
+            for u in range(2):
+                for a in range(TOKEN_TILES):
+                    nc.tensor.transpose(
+                        y_bank[:, TOKENS * u + P * a : TOKENS * u + P * (a + 1)],
+                        y_words[:, (E // 2) * a + P * u : (E // 2) * a + P * (u + 1)],
+                        ident[:],
+                    )
+            nc.vector.tensor_copy(
+                out=y_grouped[:].bitcast(F32).rearrange("p (m u) -> p m u", u=2),
+                in_=y_bank[:].rearrange("p (u m) -> p m u", u=2),
+            )
+            b1_bank = psum_tr.tile([P, 4 * P], F32, name="b1_bank", tag="tr")
+            nc.tensor.transpose(b1_bank[:, 0:P], b1_rows[:].bitcast(F32), ident[:])
+            nc.vector.tensor_copy(out=b1_col[:], in_=b1_bank[:, 0 : 2 * GROUPS].bitcast(BF16))
+            nc.vector.quantize_mx(out=y_codes[:].bitcast(FP8X4), scales=y_scales[:], in_=y_grouped[:])
 
         y_plus_b2 = const.tile([P, TOKEN_TILES * E], F32, name="y_plus_b2")
         gain = const.tile([P, E], F32, name="gain")
@@ -271,6 +286,8 @@ def tile_swintransformerblock_pb_k_kernel(tc, y, w1, b1, w2, b2, ln2_g, ln2_b, o
                 gelu(j - 1)
             if live(j - 2):
                 h_q[j - 2] = quantise(h_grouped[j - 2], TOKENS, work, "h")
+            if j == 0:
+                prepare_y_and_b1()
             if j == 1:
                 spread_vectors()
 

from contextlib import ExitStack

import concourse.mybir as mybir
from concourse.masks import make_identity

F32 = mybir.dt.float32
BF16 = mybir.dt.bfloat16
U32 = mybir.dt.uint32
U8 = mybir.dt.uint8
FP8X4 = mybir.dt.float8_e4m3fn_x4
ACT = mybir.ActivationFunctionType
ALU = mybir.AluOpType

P = 128
TOKENS = 256
E = 512
F = 16384
K_PASS = 4 * P
GROUPS = F // K_PASS
TOKEN_TILES = TOKENS // P
LN_EPS = 1e-5

W2_LAG = 2
W2_GROUPS_PER_LOAD = 2
LOADS_AHEAD = 6

FLOPS = 2 * 2 * TOKENS * E * F


def tile_swintransformerblock_pb_k_kernel(tc, y, w1, b1, w2, b2, ln2_g, ln2_b, out):
    nc = tc.nc
    with ExitStack() as ctx:
        ctx.enter_context(tc.manual_schedule())
        const = ctx.enter_context(tc.tile_pool(name="const", bufs=1))
        w1_pool = ctx.enter_context(tc.tile_pool(name="w1_pool", bufs=LOADS_AHEAD))
        w2_pool = ctx.enter_context(tc.tile_pool(name="w2_pool", bufs=4))
        work = ctx.enter_context(tc.tile_pool(name="work", bufs=3))
        psum_acc = ctx.enter_context(tc.psum_pool(name="psum_acc", bufs=1))
        psum_tr = ctx.enter_context(tc.psum_pool(name="psum_tr", bufs=4))
        psum_h = ctx.enter_context(tc.psum_pool(name="psum_h", bufs=2))

        y_view = y.rearrange("l n e -> (l n) e").rearrange("(a p) e -> p a e", p=P)
        w1_view = w1.rearrange("(g u m r) e -> g m u (r e)", u=2, m=P, r=2)
        w2_view = w2.rearrange("(j p) f -> p j f", p=P)
        b1_view = b1.rearrange("(c x) -> c x", x=2 * P)

        w1_loaded = {}
        w2_loaded = {}

        def load_round(j):
            if j < GROUPS:
                w1_sb = w1_pool.tile([P, 2 * 2 * E], BF16, name="w1_sb")
                if j == 0:
                    for u in range(2):
                        nc.sync.dma_start(out=w1_sb[:, 2 * E * u : 2 * E * (u + 1)], in_=w1_view[j][:, u, :])
                else:
                    nc.sync.dma_start(out=w1_sb[:].rearrange("p (u x) -> p u x", u=2), in_=w1_view[j])
                w1_loaded[j] = w1_sb
            g = j - W2_LAG
            if 0 <= g < GROUPS and g % W2_GROUPS_PER_LOAD == 0:
                w2_sb = w2_pool.tile([P, 4 * W2_GROUPS_PER_LOAD * K_PASS], BF16, name="w2_sb")
                w2_loaded[g // W2_GROUPS_PER_LOAD] = w2_sb
            if 0 <= g < W2_GROUPS_PER_LOAD:
                nc.sync.dma_start(
                    out=w2_loaded[0][:].rearrange("p (j f) -> p j f", j=4)[:, :, K_PASS * g : K_PASS * (g + 1)],
                    in_=w2_view[:, :, K_PASS * g : K_PASS * (g + 1)],
                )
            elif W2_GROUPS_PER_LOAD <= g < GROUPS and g % W2_GROUPS_PER_LOAD == 0:
                nc.sync.dma_start(
                    out=w2_loaded[g // W2_GROUPS_PER_LOAD][:].rearrange("p (j f) -> p j f", j=4),
                    in_=w2_view[:, :, K_PASS * g : K_PASS * (g + W2_GROUPS_PER_LOAD)],
                )

        load_round(0)
        y_sb = const.tile([P, TOKEN_TILES * E], BF16, name="y_sb")
        nc.sync.dma_start(out=y_sb[:].rearrange("p (a e) -> p a e", e=E), in_=y_view)
        for j in range(1, LOADS_AHEAD):
            load_round(j)
        b1_rows = const.tile([P, 2 * P], BF16, name="b1_rows")
        nc.vector.memset(b1_rows[:], 0.0)
        nc.scalar.dma_start(out=b1_rows[0 : F // (2 * P), :], in_=b1_view)
        vec_rows = const.tile([P, 3 * E], BF16, name="vec_rows")
        nc.vector.memset(vec_rows[:], 0.0)
        for i, vec in enumerate((b2, ln2_g, ln2_b)):
            nc.scalar.dma_start(
                out=vec_rows[0:1, E * i : E * (i + 1)], in_=vec.rearrange("(o e) -> o e", o=1)
            )
        ones = const.tile([P, P], BF16, name="ones")
        nc.vector.memset(ones[:], 1.0)
        eps = const.tile([P, 1], F32, name="eps")
        nc.vector.memset(eps[:], LN_EPS)
        ident = const.tile([P, P], F32, name="ident")
        make_identity(nc, ident[:])
        warm_gelu = const.tile([P, 1], F32, name="warm_gelu")
        nc.scalar.activation(out=warm_gelu[:], in_=eps[:], func=ACT.Gelu)

        def transpose_bank(words, starts):
            bank = psum_tr.tile([P, 4 * P], F32, name="bank", tag="tr")
            for i, start in enumerate(starts):
                nc.tensor.transpose(bank[:, P * i : P * (i + 1)], words[:, start : start + P], ident[:])
            return bank

        def copy_out(copy, grouped, quarter, bank):
            copy(
                out=grouped[:].bitcast(F32)[:, 4 * P * quarter : 4 * P * (quarter + 1)].rearrange(
                    "p (s m u) -> p s m u", s=2, u=2
                ),
                in_=bank[:].rearrange("p (s u m) -> p s m u", s=2, u=2),
            )

        def quantise(grouped, columns, pool, name):
            codes = pool.tile([P, columns], U32, name=name + "_codes", align_bytes=64)
            scales = pool.tile([P, columns], U8, name=name + "_scales", align_bytes=64)
            nc.vector.quantize_mx(out=codes[:].bitcast(FP8X4), scales=scales[:], in_=grouped[:])
            return codes, scales

        y_grouped = const.tile([P, 4 * TOKENS], BF16, name="y_grouped", align_bytes=64)
        b1_col = const.tile([P, 4 * GROUPS], F32, name="b1_col")
        y_codes = const.tile([P, TOKENS], U32, name="y_codes", align_bytes=64)
        y_scales = const.tile([P, TOKENS], U8, name="y_scales", align_bytes=64)

        def prepare_y_and_b1():
            y_words = y_sb[:].bitcast(F32)
            y_bank = psum_tr.tile([P, 4 * P], F32, name="y_bank", tag="tr")
            for u in range(2):
                for a in range(TOKEN_TILES):
                    nc.tensor.transpose(
                        y_bank[:, TOKENS * u + P * a : TOKENS * u + P * (a + 1)],
                        y_words[:, (E // 2) * a + P * u : (E // 2) * a + P * (u + 1)],
                        ident[:],
                    )
            nc.vector.tensor_copy(
                out=y_grouped[:].bitcast(F32).rearrange("p (m u) -> p m u", u=2),
                in_=y_bank[:].rearrange("p (u m) -> p m u", u=2),
            )
            b1_bank = psum_tr.tile([P, 4 * P], F32, name="b1_bank", tag="tr")
            nc.tensor.transpose(b1_bank[:, 0:P], b1_rows[:].bitcast(F32), ident[:])
            nc.vector.tensor_copy(out=b1_col[:], in_=b1_bank[:, 0 : 2 * GROUPS].bitcast(BF16))
            nc.vector.quantize_mx(out=y_codes[:].bitcast(FP8X4), scales=y_scales[:], in_=y_grouped[:])

        y_plus_b2 = const.tile([P, TOKEN_TILES * E], F32, name="y_plus_b2")
        gain = const.tile([P, E], F32, name="gain")
        shift = const.tile([P, E], F32, name="shift")

        def spread_vectors():
            spread = []
            for i in range(3):
                spread_bank = psum_tr.tile([P, E], F32, name="spread_bank", tag="tr")
                nc.tensor.matmul(
                    spread_bank[:], lhsT=ones[:], rhs=vec_rows[:, E * i : E * (i + 1)], start=True, stop=True
                )
                spread.append(spread_bank)
            for a in range(TOKEN_TILES):
                nc.vector.tensor_tensor(
                    out=y_plus_b2[:, E * a : E * (a + 1)],
                    in0=y_sb[:, E * a : E * (a + 1)],
                    in1=spread[0][:],
                    op=ALU.add,
                )
            nc.scalar.copy(out=gain[:], in_=spread[1][:])
            nc.scalar.copy(out=shift[:], in_=spread[2][:])

        acc = []
        for a in range(TOKEN_TILES):
            acc_bank = psum_acc.tile([P, E], F32, name="acc%d" % a)
            acc.append(acc_bank)

        w1_banks = {}
        w2_banks = {}
        grouped = {}
        weights_q = {}
        h_banks = {}
        h_planes = {}
        h_grouped = {}
        h_q = {}

        def transpose_w1(g):
            words = w1_loaded[g][:].bitcast(F32)
            w1_banks[g] = [transpose_bank(words, [E * u + P * i for i in range(4)]) for u in range(2)]

        def transpose_w2(g):
            c, gl = divmod(g, W2_GROUPS_PER_LOAD)
            words = w2_loaded[c][:].bitcast(F32)
            row = W2_GROUPS_PER_LOAD * K_PASS // 2
            w2_banks[g] = [
                transpose_bank(
                    words,
                    [row * (2 * half + s) + (K_PASS // 2) * gl + P * u for s in range(2) for u in range(2)],
                )
                for half in range(2)
            ]

        def quantise_weights(j):
            codes = work.tile([P, 2 * K_PASS], U32, name="w_codes", align_bytes=64)
            scales = work.tile([P, 2 * K_PASS], U8, name="w_scales", align_bytes=64)
            first = 0 if live(j) else K_PASS
            last = 2 * K_PASS if live(j - W2_LAG) else K_PASS
            nc.vector.quantize_mx(
                out=codes[:, first:last].bitcast(FP8X4),
                scales=scales[:, first:last],
                in_=grouped[j][:, 4 * first : 4 * last],
            )
            weights_q[j] = (codes, scales)

        def matmul1(g):
            codes, scales = weights_q[g]
            pair = []
            for half in range(2):
                h_bank = psum_h.tile([P, 2 * TOKENS], F32, name="h_bank", tag="hp")
                for s in range(2):
                    t = 2 * half + s
                    nc.tensor.matmul_mx(
                        out=h_bank[:, TOKENS * s : TOKENS * (s + 1)],
                        lhsT=codes[:, P * t : P * (t + 1)].bitcast(FP8X4),
                        lhsT_scale=scales[:, P * t : P * (t + 1)],
                        rhs=y_codes[:].bitcast(FP8X4),
                        rhs_scale=y_scales[:],
                        start=True,
                        stop=True,
                    )
                pair.append(h_bank)
            h_banks[g] = pair

        def gelu(g):
            planes = work.tile([P, 4 * TOKENS], BF16, name="planes")
            for t in range(4):
                nc.scalar.activation(
                    out=planes[:, TOKENS * t : TOKENS * (t + 1)],
                    in_=h_banks[g][t // 2][:, TOKENS * (t % 2) : TOKENS * (t % 2 + 1)],
                    func=ACT.Gelu,
                    bias=b1_col[:, 4 * g + t : 4 * g + t + 1],
                    scale=1.0,
                )
            h_planes[g] = planes

        def regroup(g):
            h_g = work.tile([P, 4 * TOKENS], BF16, name="h_g", align_bytes=64)
            nc.vector.tensor_copy(
                out=h_g[:].rearrange("p (c i t) -> p c t i", i=4, t=4),
                in_=h_planes[g][:].rearrange("p (t c i) -> p c t i", i=4, t=4),
            )
            h_grouped[g] = h_g

        def matmul2(g):
            h_codes, h_scales = h_q[g]
            w_codes, w_scales = weights_q[g + W2_LAG]
            for a in range(TOKEN_TILES):
                nc.tensor.matmul_mx(
                    out=acc[a][:],
                    lhsT=h_codes[:, P * a : P * (a + 1)].bitcast(FP8X4),
                    lhsT_scale=h_scales[:, P * a : P * (a + 1)],
                    rhs=w_codes[:, K_PASS : 2 * K_PASS].bitcast(FP8X4),
                    rhs_scale=w_scales[:, K_PASS : 2 * K_PASS],
                    start=(g == 0),
                    stop=(g == GROUPS - 1),
                )

        def live(g):
            return 0 <= g < GROUPS

        for j in range(GROUPS + W2_LAG + 1):
            g2 = j - W2_LAG
            if live(j):
                transpose_w1(j)
            if live(g2):
                transpose_w2(g2)
            load_round(j + LOADS_AHEAD)
            if live(j - 1) or live(g2 - 1):
                quantise_weights(j - 1)
            if live(j - 1):
                matmul1(j - 1)
            if live(g2 - 1):
                matmul2(g2 - 1)
            if live(j - 2):
                regroup(j - 2)
            if live(j) or live(g2):
                round_grouped = work.tile([P, 8 * K_PASS], BF16, name="round_grouped", align_bytes=64)
                grouped[j] = round_grouped
            if live(j):
                copy_out(nc.scalar.copy, round_grouped, 0, w1_banks[j][0])
                copy_out(nc.vector.tensor_copy, round_grouped, 1, w1_banks[j][1])
            if live(g2):
                copy_out(nc.scalar.copy, round_grouped, 2, w2_banks[g2][0])
                copy_out(nc.scalar.copy, round_grouped, 3, w2_banks[g2][1])
            if live(j - 1):
                gelu(j - 1)
            if live(j - 2):
                h_q[j - 2] = quantise(h_grouped[j - 2], TOKENS, work, "h")
            if j == 0:
                prepare_y_and_b1()
            if j == 1:
                spread_vectors()

        warm = const.tile([P, 1], F32, name="warm")
        nc.scalar.activation(out=warm[:], in_=eps[:], func=ACT.Sqrt)
        r = []
        neg_mean = []
        for a in range(TOKEN_TILES):
            r_a = const.tile([P, E], F32, name="r%d" % a)
            row_sum = const.tile([P, 1], F32, name="row_sum%d" % a)
            nc.vector.scalar_tensor_tensor(
                out=r_a[:],
                in0=acc[a][:],
                scalar=1.0,
                in1=y_plus_b2[:, E * a : E * (a + 1)],
                op0=ALU.mult,
                op1=ALU.add,
                accum_out=row_sum[:],
            )
            neg_mean_a = const.tile([P, 1], F32, name="neg_mean%d" % a)
            nc.vector.tensor_scalar(
                out=neg_mean_a[:], in0=row_sum[:], scalar1=-1.0 / E, scalar2=None, op0=ALU.mult
            )
            r.append(r_a)
            neg_mean.append(neg_mean_a)
        for a in range(TOKEN_TILES):
            squares = const.tile([P, E], F32, name="squares%d" % a)
            sum_squares = const.tile([P, 1], F32, name="sum_squares%d" % a)
            nc.scalar.activation(
                out=squares[:], in_=r[a][:], func=ACT.Square, bias=neg_mean[a][:], scale=1.0,
                accum_out=sum_squares[:],
            )
            std = const.tile([P, 1], F32, name="std%d" % a)
            nc.scalar.activation(out=std[:], in_=sum_squares[:], func=ACT.Sqrt, bias=eps[:], scale=1.0 / E)
            centred = const.tile([P, E], F32, name="centred%d" % a)
            nc.vector.scalar_tensor_tensor(
                out=centred[:], in0=r[a][:], scalar=neg_mean[a][:], in1=gain[:], op0=ALU.add, op1=ALU.mult
            )
            rstd = const.tile([P, 1], F32, name="rstd%d" % a)
            nc.vector.reciprocal(out=rstd[:], in_=std[:])
            z = const.tile([P, E], F32, name="z%d" % a)
            nc.vector.scalar_tensor_tensor(
                out=z[:], in0=centred[:], scalar=rstd[:], in1=shift[:], op0=ALU.mult, op1=ALU.add
            )
            patches = out[a].rearrange("(r w c) e -> w r c e", w=2, c=8)
            for w in range(2):
                nc.sync.dma_start(out=patches[w], in_=z[64 * w : 64 * (w + 1), :])
